import numpy as np
import ml_dtypes


def mxq(x, axis, fmt="e4m3"):
    dtype, down = {"e4m3": (ml_dtypes.float8_e4m3fn, 7), "e5m2": (ml_dtypes.float8_e5m2, 14)}[fmt]
    v = np.moveaxis(np.asarray(x, np.float32).astype(ml_dtypes.bfloat16).astype(np.float64), axis, -1)
    blocks = v.reshape(v.shape[:-1] + (-1, 32))
    amax = np.abs(blocks).max(-1, keepdims=True)
    byte = np.maximum(np.where(amax > 0, np.frexp(amax)[1] - 1 + 127, 0) - down, 1)
    scale = np.exp2(byte - 127.0)
    codes = (blocks / scale).astype(np.float32).astype(dtype).astype(np.float64)
    return np.moveaxis((codes * scale).reshape(v.shape), -1, axis)


WIDE = False


def mx_kscale(k):
    if not WIDE:
        return np.ones(k)
    levels = np.array([10, -10, 5, -5, 0])
    a = np.random.permutation(np.resize(levels, k // 512 * 4)).reshape(k // 512, 4)
    idx = np.arange(k)
    return np.exp2(a[idx // 512, idx % 128 // 32])


BF16 = ml_dtypes.bfloat16


def bf(x):
    return np.asarray(x, np.float32).astype(BF16)


def f64(x):
    return np.asarray(x).astype(np.float64)


E2M1 = np.array([0.0, 0.5, 1.0, 1.5, 2.0, 3.0, 4.0, 6.0, -0.0, -0.5, -1.0, -1.5, -2.0, -3.0, -4.0, -6.0])


def pack_weight(w, fmt):
    k, n = w.shape
    w = f64(bf(w)).reshape(k // 32, 32, n)
    amax = np.abs(w).max(1)
    if fmt == "e4m3":
        byte = np.frexp(amax)[1] - 1 + 127 - 7
    else:
        mant, ex = np.frexp(amax / 6.0)
        byte = np.where(mant > 0.5, ex, ex - 1) + 127
    byte = np.clip(np.where(amax > 0, byte, 1), 1, 254)
    scaled = (w * np.exp2(127.0 - byte)[:, None, :]).reshape(k, n).astype(np.float32)
    by_word = np.ascontiguousarray(scaled.reshape(k // 512, 128, 4, n).transpose(0, 1, 3, 2))
    if fmt == "e4m3":
        words = by_word.astype(ml_dtypes.float8_e4m3fn).view(np.uint8)
    else:
        c = by_word.astype(ml_dtypes.float4_e2m1fn).view(np.uint8) & 0xF
        words = c[..., 0::2] | (c[..., 1::2] << 4)
    return np.ascontiguousarray(words), np.ascontiguousarray(byte.astype(np.uint8).reshape(k // 512, 16, n))


def unpack_weight(words, scales, fmt):
    g, p, n, _ = words.shape
    if fmt == "e4m3":
        vals = np.ascontiguousarray(words).view(ml_dtypes.float8_e4m3fn).astype(np.float64)
    else:
        nib = np.empty((g, p, n, 4), np.uint8)
        nib[..., 0::2] = words & 0xF
        nib[..., 1::2] = words >> 4
        vals = E2M1[nib]
    vals = vals * np.repeat(np.exp2(scales.astype(np.float64) - 127.0), 8, axis=1)[..., None]
    return vals.transpose(0, 1, 3, 2).reshape(g * 512, n)

def pack4(w):
    words, scales = pack_weight(w, "e2m1")
    return words.reshape(words.shape[0], 128, -1), scales


def unpack4(words, scales):
    return unpack_weight(words.reshape(words.shape[0], 128, -1, 2), scales, "e2m1")


B, S, E, H = 2, 256, 512, 4
D = E // H
LN_EPS = 1e-6


def setup_inputs():
    s = mx_kscale(E)
    h_attn = bf(np.random.standard_normal((B, H, S, D)) * 0.4 * s.reshape(H, 1, D))
    x = bf(np.random.standard_normal((B, S, E)))
    out_w_words, out_w_scales = pack4(np.random.standard_normal((E, E)) * 2.0 / np.sqrt(E) / s[:, None])
    ln_gamma = bf(1.0 + 0.1 * np.random.standard_normal(E))
    ln_beta = bf(0.1 * np.random.standard_normal(E))
    return {"h_attn": h_attn,
            "x": x,
            "out_w_words": out_w_words,
            "out_w_scales": out_w_scales,
            "ln_gamma": ln_gamma,
            "ln_beta": ln_beta}


def reference(h_attn, x, out_w_words, out_w_scales, ln_gamma, ln_beta):
    merged = f64(h_attn).transpose(0, 2, 1, 3).reshape(B, S, E)
    out = mxq(merged, 2, "e4m3") @ unpack4(out_w_words, out_w_scales)
    y = out + f64(x)
    mean = y.mean(-1, keepdims=True)
    var = np.square(y - mean).mean(-1, keepdims=True)
    return (y - mean) / np.sqrt(var + LN_EPS) * f64(ln_gamma) + f64(ln_beta)

@@ -1,0 +1,252 @@
+from contextlib import ExitStack
+
+import concourse.mybir as mybir
+from concourse.masks import make_identity
+
+F32 = mybir.dt.float32
+BF16 = mybir.dt.bfloat16
+I32 = mybir.dt.int32
+U32 = mybir.dt.uint32
+U8 = mybir.dt.uint8
+FP8X4 = mybir.dt.float8_e4m3fn_x4
+FP4X4 = mybir.dt.float4_e2m1fn_x4
+ALU = mybir.AluOpType
+ACT = mybir.ActivationFunctionType
+
+P = 128
+B, H, S, D = 2, 4, 256, 128
+E = H * D
+S_BLOCKS = S // P
+TILES = B * S_BLOCKS
+WORDS = E // 2
+E_CHUNKS = E // P
+LN_EPS = 1e-6
+GPSIMD_TILES = (1, 3)
+
+WARM_COLS = 256
+WARM_PASSES = 2
+
+FLOPS = 2 * B * S * E * E
+
+
+def tile_selfattention_pa_s_kernel(tc, h_attn, x, out_w_words, out_w_scales, ln_gamma, ln_beta, out):
+    nc = tc.nc
+    with ExitStack() as ctx:
+        ctx.enter_context(tc.manual_schedule())
+        keep = ctx.enter_context(tc.tile_pool(name="keep", bufs=1))
+        work = ctx.enter_context(tc.tile_pool(name="work", bufs=TILES))
+        psum = ctx.enter_context(tc.psum_pool(name="psum", bufs=TILES))
+        psum_gb = ctx.enter_context(tc.psum_pool(name="psum_gb", bufs=1))
+
+        h_sb = keep.tile([P, TILES, E], BF16)
+        x_sb = keep.tile([P, TILES, E], BF16)
+        w_words = keep.tile([P, 2 * E], U8, align_bytes=64)
+        w_plane = keep.tile([P, E], U8, align_bytes=64)
+        gb_rows = keep.tile([P, P], BF16)
+        ident = keep.tile([P, P], F32)
+        ident_bf = keep.tile([P, P], BF16)
+        one = keep.tile([P, 1], F32)
+        warm = keep.tile([P, 1], F32)
+
+        zeros = keep.tile([P, WARM_COLS], F32)
+        nc.vector.memset(zeros[:], 0.0)
+        scratch = psum_gb.tile([P, WARM_COLS], F32)
+        for i in range(WARM_PASSES):
+            nc.tensor.matmul(out=scratch[:], lhsT=zeros[:, 0:P], rhs=zeros[:], start=True, stop=True)
+
+        nc.vector.memset(w_plane[:].bitcast(I32), 0)
+        for j in range(S_BLOCKS):
+            nc.sync.dma_start(
+                out=h_sb[:, B * j : B * (j + 1), :].rearrange("p t (h d) -> p (t h) d", d=D),
+                in_=h_attn[:, :, j * P : (j + 1) * P, :].rearrange("b h s d -> s (b h) d"),
+            )
+        nc.sync.dma_start(out=w_words[:].bitcast(I32), in_=out_w_words[0].bitcast(I32))
+        for r in range(4):
+            nc.sync.dma_start(out=w_plane[r:P:32, :].bitcast(I32), in_=out_w_scales[0, r:16:4, :].bitcast(I32))
+        for j in range(S_BLOCKS):
+            nc.sync.dma_start(
+                out=x_sb[:, B * j : B * (j + 1), :],
+                in_=x[:, j * P : (j + 1) * P, :].rearrange("b s e -> s b e"),
+            )
+        gamma_sb = keep.tile([P, E], BF16)
+        nc.sync.dma_start(out=gamma_sb[:], in_=ln_gamma.partition_broadcast(P))
+        make_identity(nc, ident[:])
+        nc.gpsimd.memset(gb_rows[:], 0.0)
+        nc.gpsimd.dma_start(out=gb_rows[0:E_CHUNKS, :], in_=ln_gamma.rearrange("(c k) -> c k", k=P))
+        nc.gpsimd.dma_start(out=gb_rows[E_CHUNKS : 2 * E_CHUNKS, :], in_=ln_beta.rearrange("(c k) -> c k", k=P))
+        nc.vector.memset(one[:], 1.0)
+        nc.vector.tensor_copy(out=ident_bf[:], in_=ident[:])
+        nc.scalar.activation(out=warm[:], in_=one[:], func=ACT.Abs_reciprocal_sqrt)
+
+        banks = []
+        codes_of = []
+
+        def transpose_tile(t):
+            bank = psum.tile([P, E], F32)
+            h_words = h_sb[:, t, :].bitcast(F32)
+            for u in range(2):
+                nc.tensor.transpose(bank[:, u * P : (u + 1) * P], h_words[:, u:WORDS:2], ident[:])
+            banks.append(bank)
+
+        def quantise(t):
+            grouped = work.tile([P, 4 * P], BF16, align_bytes=64)
+            nc.scalar.copy(
+                out=grouped[:].bitcast(F32).rearrange("p (r u) -> p r u", u=2),
+                in_=banks[t][:, 0 : 2 * P].rearrange("p (u r) -> p r u", u=2),
+            )
+            m_codes = work.tile([P, P], U32, align_bytes=64)
+            m_scales = work.tile([P, P], U8, align_bytes=64)
+            nc.vector.quantize_mx(out=m_codes[:].bitcast(FP8X4), scales=m_scales[:], in_=grouped[:])
+            codes_of.append((m_codes, m_scales))
+
+        def multiply(t):
+            m_codes, m_scales = codes_of[t]
+            nc.tensor.matmul_mx(
+                out=banks[t][:],
+                lhsT=m_codes[:].bitcast(FP8X4),
+                lhsT_scale=m_scales[:],
+                rhs=w_words[:].bitcast(FP4X4),
+                rhs_scale=w_plane[:],
+                start=True,
+                stop=True,
+            )
+
+        gb_t = psum_gb.tile([P, P], BF16)
+        gb_cols = keep.tile([P, 2 * E_CHUNKS], BF16)
+        gamma_all = psum_gb.tile([P, E], BF16)
+        beta_all = psum_gb.tile([P, E], BF16)
+
+        y_sum = keep.tile([P, TILES], F32)
+        neg_mean = keep.tile([P, TILES], F32)
+        sq_sum = keep.tile([P, TILES], F32)
+        rstd = keep.tile([P, TILES], F32)
+        ys = []
+        shifted_of = {}
+        centred_of = {}
+
+        def add_residual(t):
+            y = work.tile([P, E], F32)
+            nc.vector.scalar_tensor_tensor(
+                out=y[:],
+                in0=banks[t][:],
+                scalar=-1.0 if t in GPSIMD_TILES else 1.0,
+                in1=x_sb[:, t, :],
+                op0=ALU.mult,
+                op1=ALU.subtract if t in GPSIMD_TILES else ALU.add,
+                accum_out=y_sum[:, t : t + 1],
+            )
+            ys.append(y)
+
+        def shift(t):
+            shifted = work.tile([P, E], F32)
+            nc.scalar.activation(
+                out=shifted[:], in_=ys[t][:], func=ACT.Identity, bias=y_sum[:, t : t + 1], scale=-1.0 * E
+            )
+            shifted_of[t] = shifted
+
+        def sum_squares(t):
+            squares = work.tile([P, E], F32)
+            nc.scalar.activation(
+                out=squares[:],
+                in_=ys[t][:],
+                func=ACT.Square,
+                bias=y_sum[:, t : t + 1],
+                scale=-1.0 * E,
+                accum_out=sq_sum[:, t : t + 1],
+            )
+
+        def inverse_deviation(t0, t1):
+            nc.scalar.activation(
+                out=rstd[:, t0:t1],
+                in_=sq_sum[:, t0:t1],
+                func=ACT.Abs_reciprocal_sqrt,
+                bias=LN_EPS * E * E,
+                scale=1.0 / E,
+            )
+
+        def minus_mean(t):
+            nc.gpsimd.tensor_scalar(
+                out=neg_mean[:, t : t + 1],
+                in0=y_sum[:, t : t + 1],
+                scalar1=-1.0 / E,
+                scalar2=0.0,
+                op0=ALU.mult,
+                op1=ALU.add,
+            )
+
+        def centre(t):
+            centred = work.tile([P, E], F32)
+            if t in GPSIMD_TILES:
+                nc.gpsimd.tensor_tensor(out=centred[:], in0=shifted_of[t][:], in1=gamma_sb[:], op=ALU.mult)
+            else:
+                nc.vector.scalar_tensor_tensor(
+                    out=centred[:],
+                    in0=ys[t][:],
+                    scalar=neg_mean[:, t : t + 1],
+                    in1=gamma_all[:],
+                    op0=ALU.add,
+                    op1=ALU.mult,
+                )
+            centred_of[t] = centred
+
+        def finish(t):
+            j, b = divmod(t, B)
+            result = work.tile([P, E], F32)
+            pieces = 2 if t == TILES - 1 else 1
+            width = E // pieces
+            for c in range(pieces):
+                cols = slice(c * width, (c + 1) * width)
+                nc.vector.scalar_tensor_tensor(
+                    out=result[:, cols],
+                    in0=centred_of[t][:, cols],
+                    scalar=rstd[:, t : t + 1],
+                    in1=beta_all[:, cols],
+                    op0=ALU.mult,
+                    op1=ALU.add,
+                )
+                nc.sync.dma_start(out=out[b, j * P : (j + 1) * P, cols], in_=result[:, cols])
+
+        for t in range(TILES):
+            transpose_tile(t)
+        quantise(0)
+        multiply(0)
+        quantise(1)
+        multiply(1)
+        nc.tensor.transpose(gb_t[:], gb_rows[:], ident_bf[:])
+        quantise(2)
+        multiply(2)
+        add_residual(0)
+        minus_mean(0)
+        quantise(3)
+        multiply(3)
+        nc.scalar.activation(out=gb_cols[:, 0:E_CHUNKS], in_=gb_t[:, 0:E_CHUNKS], func=ACT.Copy, scale=1.0 * E)
+        nc.scalar.copy(out=gb_cols[:, E_CHUNKS : 2 * E_CHUNKS], in_=gb_t[:, E_CHUNKS : 2 * E_CHUNKS])
+        for c in range(E_CHUNKS):
+            nc.tensor.transpose(
+                gamma_all[:, c * P : (c + 1) * P], gb_cols[:, c : c + 1].to_broadcast([P, P]), ident_bf[:]
+            )
+        for c in range(E_CHUNKS):
+            nc.tensor.transpose(
+                beta_all[:, c * P : (c + 1) * P],
+                gb_cols[:, E_CHUNKS + c : E_CHUNKS + c + 1].to_broadcast([P, P]),
+                ident_bf[:],
+            )
+        sum_squares(0)
+        add_residual(1)
+        shift(1)
+        sum_squares(1)
+        add_residual(2)
+        minus_mean(2)
+        centre(1)
+        add_residual(3)
+        shift(3)
+        inverse_deviation(0, 2)
+        sum_squares(2)
+        inverse_deviation(2, 3)
+        sum_squares(3)
+        inverse_deviation(3, 4)
+        centre(3)
+        centre(0)
+        centre(2)
+        for t in range(TILES):
+            finish(t)

@@ -21,7 +21,7 @@ TILES = B * S_BLOCKS
 WORDS = E // 2
 E_CHUNKS = E // P
 LN_EPS = 1e-6
-GPSIMD_TILES = (1, 3)
+GPSIMD_TILES = (0, 2)
 
 WARM_COLS = 256
 WARM_PASSES = 2
@@ -216,7 +216,6 @@ def tile_selfattention_pa_s_kernel(tc, h_attn, x, out_w_words, out_w_scales, ln_
         quantise(2)
         multiply(2)
         add_residual(0)
-        minus_mean(0)
         quantise(3)
         multiply(3)
         nc.scalar.activation(out=gb_cols[:, 0:E_CHUNKS], in_=gb_t[:, 0:E_CHUNKS], func=ACT.Copy, scale=1.0 * E)
@@ -231,22 +230,26 @@ def tile_selfattention_pa_s_kernel(tc, h_attn, x, out_w_words, out_w_scales, ln_
                 gb_cols[:, E_CHUNKS + c : E_CHUNKS + c + 1].to_broadcast([P, P]),
                 ident_bf[:],
             )
-        sum_squares(0)
+        shift(0)
         add_residual(1)
-        shift(1)
-        sum_squares(1)
+        sum_squares(0)
+        minus_mean(1)
         add_residual(2)
-        minus_mean(2)
-        centre(1)
+        sum_squares(1)
+        centre(0)
         add_residual(3)
-        shift(3)
-        inverse_deviation(0, 2)
+        inverse_deviation(0, 1)
+        shift(2)
+        inverse_deviation(1, 2)
+        minus_mean(3)
         sum_squares(2)
+        centre(2)
+        centre(1)
+        finish(0)
         inverse_deviation(2, 3)
         sum_squares(3)
         inverse_deviation(3, 4)
+        finish(1)
         centre(3)
-        centre(0)
-        centre(2)
-        for t in range(TILES):
-            finish(t)
+        finish(2)
+        finish(3)

@@ -128,9 +128,9 @@ def tile_selfattention_pa_s_kernel(tc, h_attn, x, out_w_words, out_w_scales, ln_
             y = work.tile([P, E], F32)
             nc.vector.scalar_tensor_tensor(
                 out=y[:],
-                in0=banks[t][:],
+                in0=x_sb[:, t, :],
                 scalar=-1.0 if t in GPSIMD_TILES else 1.0,
-                in1=x_sb[:, t, :],
+                in1=banks[t][:],
                 op0=ALU.mult,
                 op1=ALU.subtract if t in GPSIMD_TILES else ALU.add,
                 accum_out=y_sum[:, t : t + 1],

@@ -42,7 +42,8 @@ def tile_selfattention_pa_s_kernel(tc, h_attn, x, out_w_words, out_w_scales, ln_
         x_sb = keep.tile([P, TILES, E], BF16)
         w_words = keep.tile([P, 2 * E], U8, align_bytes=64)
         w_plane = keep.tile([P, E], U8, align_bytes=64)
-        gb_rows = keep.tile([P, P], BF16)
+        gamma_rows = keep.tile([P, P], BF16)
+        beta_rows = keep.tile([P, P], BF16)
         ident = keep.tile([P, P], F32)
         ident_bf = keep.tile([P, P], BF16)
         one = keep.tile([P, 1], F32)
@@ -55,11 +56,20 @@ def tile_selfattention_pa_s_kernel(tc, h_attn, x, out_w_words, out_w_scales, ln_
             nc.tensor.matmul(out=scratch[:], lhsT=zeros[:, 0:P], rhs=zeros[:], start=True, stop=True)
 
         nc.vector.memset(w_plane[:].bitcast(I32), 0)
-        for j in range(S_BLOCKS):
+        nc.gpsimd.memset(gamma_rows[:], 0.0)
+        make_identity(nc, ident[:])
+        nc.gpsimd.memset(beta_rows[:], 0.0)
+        nc.gpsimd.dma_start(out=beta_rows[0:E_CHUNKS, :], in_=ln_beta.rearrange("(c k) -> c k", k=P))
+
+        def load_h(j):
             nc.sync.dma_start(
                 out=h_sb[:, B * j : B * (j + 1), :].rearrange("p t (h d) -> p (t h) d", d=D),
                 in_=h_attn[:, :, j * P : (j + 1) * P, :].rearrange("b h s d -> s (b h) d"),
             )
+
+        load_h(0)
+        nc.sync.dma_start(out=gamma_rows[0:E_CHUNKS, :], in_=ln_gamma.rearrange("(c k) -> c k", k=P))
+        load_h(1)
         nc.sync.dma_start(out=w_words[:].bitcast(I32), in_=out_w_words[0].bitcast(I32))
         for r in range(4):
             nc.sync.dma_start(out=w_plane[r:P:32, :].bitcast(I32), in_=out_w_scales[0, r:16:4, :].bitcast(I32))
@@ -69,11 +79,6 @@ def tile_selfattention_pa_s_kernel(tc, h_attn, x, out_w_words, out_w_scales, ln_
                 in_=x[:, j * P : (j + 1) * P, :].rearrange("b s e -> s b e"),
             )
         gamma_sb = keep.tile([P, E], BF16)
-        nc.sync.dma_start(out=gamma_sb[:], in_=ln_gamma.partition_broadcast(P))
-        make_identity(nc, ident[:])
-        nc.gpsimd.memset(gb_rows[:], 0.0)
-        nc.gpsimd.dma_start(out=gb_rows[0:E_CHUNKS, :], in_=ln_gamma.rearrange("(c k) -> c k", k=P))
-        nc.gpsimd.dma_start(out=gb_rows[E_CHUNKS : 2 * E_CHUNKS, :], in_=ln_beta.rearrange("(c k) -> c k", k=P))
         nc.vector.memset(one[:], 1.0)
         nc.vector.tensor_copy(out=ident_bf[:], in_=ident[:])
         nc.scalar.activation(out=warm[:], in_=one[:], func=ACT.Abs_reciprocal_sqrt)
@@ -111,10 +116,21 @@ def tile_selfattention_pa_s_kernel(tc, h_attn, x, out_w_words, out_w_scales, ln_
                 stop=True,
             )
 
-        gb_t = psum_gb.tile([P, P], BF16)
-        gb_cols = keep.tile([P, 2 * E_CHUNKS], BF16)
+        rows_t = psum_gb.tile([P, 2, P], BF16)
+        gamma_cols = keep.tile([P, E_CHUNKS], BF16)
+        beta_cols = keep.tile([P, E_CHUNKS], BF16)
         gamma_all = psum_gb.tile([P, E], BF16)
         beta_all = psum_gb.tile([P, E], BF16)
+
+        def transpose_rows(i, rows):
+            nc.tensor.transpose(rows_t[:, i, :], rows[:], ident_bf[:])
+
+        def columns(i, cols):
+            nc.scalar.copy(out=cols[:], in_=rows_t[:, i, 0:E_CHUNKS])
+
+        def spread(dst, cols):
+            for c in range(E_CHUNKS):
+                nc.tensor.transpose(dst[:, c * P : (c + 1) * P], cols[:, c : c + 1].to_broadcast([P, P]), ident_bf[:])
 
         y_sum = keep.tile([P, TILES], F32)
         neg_mean = keep.tile([P, TILES], F32)
@@ -155,13 +171,14 @@ def tile_selfattention_pa_s_kernel(tc, h_attn, x, out_w_words, out_w_scales, ln_
                 accum_out=sq_sum[:, t : t + 1],
             )
 
-        def inverse_deviation(t0, t1):
+        def inverse_deviation(t):
+            factor = E if t in GPSIMD_TILES else 1
             nc.scalar.activation(
-                out=rstd[:, t0:t1],
-                in_=sq_sum[:, t0:t1],
+                out=rstd[:, t : t + 1],
+                in_=sq_sum[:, t : t + 1],
                 func=ACT.Abs_reciprocal_sqrt,
-                bias=LN_EPS * E * E,
-                scale=1.0 / E,
+                bias=LN_EPS * factor * factor,
+                scale=float(factor * factor) / (E * E * E),
             )
 
         def minus_mean(t):
@@ -206,49 +223,45 @@ def tile_selfattention_pa_s_kernel(tc, h_attn, x, out_w_words, out_w_scales, ln_
                 )
                 nc.sync.dma_start(out=out[b, j * P : (j + 1) * P, cols], in_=result[:, cols])
 
-        for t in range(TILES):
-            transpose_tile(t)
+        transpose_rows(0, gamma_rows)
+        columns(0, gamma_cols)
+        transpose_tile(0)
+        transpose_tile(1)
+        spread(gamma_all, gamma_cols)
+        transpose_tile(2)
+        transpose_tile(3)
         quantise(0)
         multiply(0)
         quantise(1)
         multiply(1)
-        nc.tensor.transpose(gb_t[:], gb_rows[:], ident_bf[:])
+        transpose_rows(1, beta_rows)
         quantise(2)
         multiply(2)
         add_residual(0)
         quantise(3)
         multiply(3)
-        nc.scalar.activation(out=gb_cols[:, 0:E_CHUNKS], in_=gb_t[:, 0:E_CHUNKS], func=ACT.Copy, scale=1.0 * E)
-        nc.scalar.copy(out=gb_cols[:, E_CHUNKS : 2 * E_CHUNKS], in_=gb_t[:, E_CHUNKS : 2 * E_CHUNKS])
-        for c in range(E_CHUNKS):
-            nc.tensor.transpose(
-                gamma_all[:, c * P : (c + 1) * P], gb_cols[:, c : c + 1].to_broadcast([P, P]), ident_bf[:]
-            )
-        for c in range(E_CHUNKS):
-            nc.tensor.transpose(
-                beta_all[:, c * P : (c + 1) * P],
-                gb_cols[:, E_CHUNKS + c : E_CHUNKS + c + 1].to_broadcast([P, P]),
-                ident_bf[:],
-            )
+        nc.scalar.copy(out=gamma_sb[:], in_=gamma_all[:])
+        columns(1, beta_cols)
+        spread(beta_all, beta_cols)
         shift(0)
         add_residual(1)
         sum_squares(0)
         minus_mean(1)
         add_residual(2)
+        inverse_deviation(0)
         sum_squares(1)
         centre(0)
         add_residual(3)
-        inverse_deviation(0, 1)
         shift(2)
-        inverse_deviation(1, 2)
+        inverse_deviation(1)
         minus_mean(3)
         sum_squares(2)
         centre(2)
         centre(1)
         finish(0)
-        inverse_deviation(2, 3)
+        inverse_deviation(2)
         sum_squares(3)
-        inverse_deviation(3, 4)
+        inverse_deviation(3)
         finish(1)
         centre(3)
         finish(2)

@@ -16,12 +16,12 @@ ACT = mybir.ActivationFunctionType
 P = 128
 B, H, S, D = 2, 4, 256, 128
 E = H * D
-S_BLOCKS = S // P
-TILES = B * S_BLOCKS
+R = S // P
+TILES = B * R
 WORDS = E // 2
 E_CHUNKS = E // P
 LN_EPS = 1e-6
-GPSIMD_TILES = (0, 2)
+GPSIMD_TILES = (1, 3)
 
 WARM_COLS = 256
 WARM_PASSES = 2
@@ -38,7 +38,8 @@ def tile_selfattention_pa_s_kernel(tc, h_attn, x, out_w_words, out_w_scales, ln_
         psum = ctx.enter_context(tc.psum_pool(name="psum", bufs=TILES))
         psum_gb = ctx.enter_context(tc.psum_pool(name="psum_gb", bufs=1))
 
-        h_sb = keep.tile([P, TILES, E], BF16)
+        h_sb = keep.tile([P, B, H, R * D], BF16)
+        h_words = keep.tile([P, TILES, WORDS], F32)
         x_sb = keep.tile([P, TILES, E], BF16)
         w_words = keep.tile([P, 2 * E], U8, align_bytes=64)
         w_plane = keep.tile([P, E], U8, align_bytes=64)
@@ -62,10 +63,7 @@ def tile_selfattention_pa_s_kernel(tc, h_attn, x, out_w_words, out_w_scales, ln_
         nc.gpsimd.dma_start(out=beta_rows[0:E_CHUNKS, :], in_=ln_beta.rearrange("(c k) -> c k", k=P))
 
         def load_h(j):
-            nc.sync.dma_start(
-                out=h_sb[:, B * j : B * (j + 1), :].rearrange("p t (h d) -> p (t h) d", d=D),
-                in_=h_attn[:, :, j * P : (j + 1) * P, :].rearrange("b h s d -> s (b h) d"),
-            )
+            nc.sync.dma_start(out=h_sb[:, j], in_=h_attn[j].rearrange("h (p r) d -> p h (r d)", r=R))
 
         load_h(0)
         nc.sync.dma_start(out=gamma_rows[0:E_CHUNKS, :], in_=ln_gamma.rearrange("(c k) -> c k", k=P))
@@ -73,10 +71,10 @@ def tile_selfattention_pa_s_kernel(tc, h_attn, x, out_w_words, out_w_scales, ln_
         nc.sync.dma_start(out=w_words[:].bitcast(I32), in_=out_w_words[0].bitcast(I32))
         for r in range(4):
             nc.sync.dma_start(out=w_plane[r:P:32, :].bitcast(I32), in_=out_w_scales[0, r:16:4, :].bitcast(I32))
-        for j in range(S_BLOCKS):
+        for j in range(B):
             nc.sync.dma_start(
-                out=x_sb[:, B * j : B * (j + 1), :],
-                in_=x[:, j * P : (j + 1) * P, :].rearrange("b s e -> s b e"),
+                out=x_sb[:, R * j : R * (j + 1), :].rearrange("p r e -> p (r e)"),
+                in_=x[j].rearrange("(p r) e -> p (r e)", r=R),
             )
         gamma_sb = keep.tile([P, E], BF16)
         nc.vector.memset(one[:], 1.0)
@@ -86,11 +84,17 @@ def tile_selfattention_pa_s_kernel(tc, h_attn, x, out_w_words, out_w_scales, ln_
         banks = []
         codes_of = []
 
+        def gather_words(t):
+            b, r = divmod(t, R)
+            nc.vector.tensor_copy(
+                out=h_words[:, t, :].rearrange("p (u h i) -> p u h i", u=2, h=H),
+                in_=h_sb[:, b, :, r * D : (r + 1) * D].bitcast(F32).rearrange("p h (i u) -> p u h i", u=2),
+            )
+
         def transpose_tile(t):
             bank = psum.tile([P, E], F32)
-            h_words = h_sb[:, t, :].bitcast(F32)
             for u in range(2):
-                nc.tensor.transpose(bank[:, u * P : (u + 1) * P], h_words[:, u:WORDS:2], ident[:])
+                nc.tensor.transpose(bank[:, u * P : (u + 1) * P], h_words[:, t, u * P : (u + 1) * P], ident[:])
             banks.append(bank)
 
         def quantise(t):
@@ -207,7 +211,7 @@ def tile_selfattention_pa_s_kernel(tc, h_attn, x, out_w_words, out_w_scales, ln_
             centred_of[t] = centred
 
         def finish(t):
-            j, b = divmod(t, B)
+            b, r = divmod(t, R)
             result = work.tile([P, E], F32)
             pieces = 2 if t == TILES - 1 else 1
             width = E // pieces
@@ -221,48 +225,52 @@ def tile_selfattention_pa_s_kernel(tc, h_attn, x, out_w_words, out_w_scales, ln_
                     op0=ALU.mult,
                     op1=ALU.add,
                 )
-                nc.sync.dma_start(out=out[b, j * P : (j + 1) * P, cols], in_=result[:, cols])
+                nc.sync.dma_start(out=out[b].rearrange("(p r) e -> p r e", r=R)[:, r, cols], in_=result[:, cols])
 
+        gather_words(0)
+        gather_words(1)
+        gather_words(2)
+        gather_words(3)
+        transpose_tile(0)
+        quantise(0)
         transpose_rows(0, gamma_rows)
         columns(0, gamma_cols)
-        transpose_tile(0)
         transpose_tile(1)
-        spread(gamma_all, gamma_cols)
         transpose_tile(2)
         transpose_tile(3)
-        quantise(0)
-        multiply(0)
+        spread(gamma_all, gamma_cols)
         quantise(1)
+        quantise(2)
+        quantise(3)
+        nc.scalar.copy(out=gamma_sb[:], in_=gamma_all[:])
+        multiply(0)
         multiply(1)
         transpose_rows(1, beta_rows)
-        quantise(2)
         multiply(2)
-        add_residual(0)
-        quantise(3)
         multiply(3)
-        nc.scalar.copy(out=gamma_sb[:], in_=gamma_all[:])
+        add_residual(0)
+        minus_mean(0)
+        sum_squares(0)
         columns(1, beta_cols)
         spread(beta_all, beta_cols)
-        shift(0)
         add_residual(1)
-        sum_squares(0)
-        minus_mean(1)
-        add_residual(2)
+        shift(1)
         inverse_deviation(0)
         sum_squares(1)
+        add_residual(2)
+        minus_mean(2)
+        centre(1)
+        sum_squares(2)
         centre(0)
         add_residual(3)
-        shift(2)
+        shift(3)
         inverse_deviation(1)
-        minus_mean(3)
-        sum_squares(2)
-        centre(2)
-        centre(1)
-        finish(0)
         inverse_deviation(2)
         sum_squares(3)
         inverse_deviation(3)
-        finish(1)
         centre(3)
+        finish(0)
+        centre(2)
+        finish(1)
         finish(2)
         finish(3)

@@ -21,7 +21,9 @@ TILES = B * R
 WORDS = E // 2
 E_CHUNKS = E // P
 LN_EPS = 1e-6
-GPSIMD_TILES = (1, 3)
+GPSIMD_TILES = (0, 1)
+SHARED_TILE = 3
+SHARE = E // 2
 
 WARM_COLS = 256
 WARM_PASSES = 2
@@ -159,10 +161,19 @@ def tile_selfattention_pa_s_kernel(tc, h_attn, x, out_w_words, out_w_scales, ln_
 
         def shift(t):
             shifted = work.tile([P, E], F32)
+            shifted_of[t] = shifted
+            if t == SHARED_TILE:
+                nc.scalar.activation(
+                    out=shifted[:, 0:SHARE],
+                    in_=ys[t][:, 0:SHARE],
+                    func=ACT.Identity,
+                    bias=neg_mean[:, t : t + 1],
+                    scale=1.0,
+                )
+                return
             nc.scalar.activation(
                 out=shifted[:], in_=ys[t][:], func=ACT.Identity, bias=y_sum[:, t : t + 1], scale=-1.0 * E
             )
-            shifted_of[t] = shifted
 
         def sum_squares(t):
             squares = work.tile([P, E], F32)
@@ -186,29 +197,27 @@ def tile_selfattention_pa_s_kernel(tc, h_attn, x, out_w_words, out_w_scales, ln_
             )
 
         def minus_mean(t):
-            nc.gpsimd.tensor_scalar(
-                out=neg_mean[:, t : t + 1],
-                in0=y_sum[:, t : t + 1],
-                scalar1=-1.0 / E,
-                scalar2=0.0,
-                op0=ALU.mult,
-                op1=ALU.add,
+            nc.scalar.activation(
+                out=neg_mean[:, t : t + 1], in_=y_sum[:, t : t + 1], func=ACT.Copy, scale=-1.0 / E
             )
 
         def centre(t):
             centred = work.tile([P, E], F32)
-            if t in GPSIMD_TILES:
-                nc.gpsimd.tensor_tensor(out=centred[:], in0=shifted_of[t][:], in1=gamma_sb[:], op=ALU.mult)
-            else:
+            centred_of[t] = centred
+            own = E if t in GPSIMD_TILES else SHARE if t == SHARED_TILE else 0
+            if own:
+                nc.gpsimd.tensor_tensor(
+                    out=centred[:, 0:own], in0=shifted_of[t][:, 0:own], in1=gamma_sb[:, 0:own], op=ALU.mult
+                )
+            if own < E:
                 nc.vector.scalar_tensor_tensor(
-                    out=centred[:],
-                    in0=ys[t][:],
+                    out=centred[:, own:E],
+                    in0=ys[t][:, own:E],
                     scalar=neg_mean[:, t : t + 1],
-                    in1=gamma_all[:],
+                    in1=gamma_all[:, own:E],
                     op0=ALU.add,
                     op1=ALU.mult,
                 )
-            centred_of[t] = centred
 
         def finish(t):
             b, r = divmod(t, R)
@@ -240,37 +249,38 @@ def tile_selfattention_pa_s_kernel(tc, h_attn, x, out_w_words, out_w_scales, ln_
         transpose_tile(3)
         spread(gamma_all, gamma_cols)
         quantise(1)
-        quantise(2)
-        quantise(3)
-        nc.scalar.copy(out=gamma_sb[:], in_=gamma_all[:])
         multiply(0)
         multiply(1)
         transpose_rows(1, beta_rows)
+        quantise(2)
         multiply(2)
-        multiply(3)
         add_residual(0)
-        minus_mean(0)
-        sum_squares(0)
+        quantise(3)
+        multiply(3)
+        nc.scalar.copy(out=gamma_sb[:], in_=gamma_all[:])
         columns(1, beta_cols)
         spread(beta_all, beta_cols)
+        shift(0)
+        centre(0)
         add_residual(1)
+        sum_squares(0)
         shift(1)
-        inverse_deviation(0)
-        sum_squares(1)
+        centre(1)
         add_residual(2)
         minus_mean(2)
-        centre(1)
-        sum_squares(2)
-        centre(0)
+        inverse_deviation(0)
         add_residual(3)
+        sum_squares(2)
+        minus_mean(3)
+        centre(2)
+        finish(0)
+        inverse_deviation(2)
+        sum_squares(1)
         shift(3)
         inverse_deviation(1)
-        inverse_deviation(2)
         sum_squares(3)
         inverse_deviation(3)
-        centre(3)
-        finish(0)
-        centre(2)
-        finish(1)
         finish(2)
+        finish(1)
+        centre(3)
         finish(3)

@@ -55,8 +55,12 @@ def tile_selfattention_pa_s_kernel(tc, h_attn, x, out_w_words, out_w_scales, ln_
         zeros = keep.tile([P, WARM_COLS], F32)
         nc.vector.memset(zeros[:], 0.0)
         scratch = psum_gb.tile([P, WARM_COLS], F32)
-        for i in range(WARM_PASSES):
+
+        def keep_clock():
             nc.tensor.matmul(out=scratch[:], lhsT=zeros[:, 0:P], rhs=zeros[:], start=True, stop=True)
+
+        for i in range(WARM_PASSES):
+            keep_clock()
 
         nc.vector.memset(w_plane[:].bitcast(I32), 0)
         nc.gpsimd.memset(gamma_rows[:], 0.0)
@@ -88,10 +92,12 @@ def tile_selfattention_pa_s_kernel(tc, h_attn, x, out_w_words, out_w_scales, ln_
 
         def gather_words(t):
             b, r = divmod(t, R)
-            nc.vector.tensor_copy(
-                out=h_words[:, t, :].rearrange("p (u h i) -> p u h i", u=2, h=H),
-                in_=h_sb[:, b, :, r * D : (r + 1) * D].bitcast(F32).rearrange("p h (i u) -> p u h i", u=2),
-            )
+            words = h_sb[:, b, :, r * D : (r + 1) * D].bitcast(F32)
+            for u in range(2):
+                nc.vector.tensor_copy(
+                    out=h_words[:, t, u * P : (u + 1) * P].rearrange("p (h i) -> p h i", h=H),
+                    in_=words[:, :, u : WORDS // H : 2],
+                )
 
         def transpose_tile(t):
             bank = psum.tile([P, E], F32)
@@ -245,6 +251,7 @@ def tile_selfattention_pa_s_kernel(tc, h_attn, x, out_w_words, out_w_scales, ln_
         transpose_rows(0, gamma_rows)
         columns(0, gamma_cols)
         transpose_tile(1)
+        keep_clock()
         transpose_tile(2)
         transpose_tile(3)
         spread(gamma_all, gamma_cols)

@@ -66,7 +66,6 @@ def tile_selfattention_pa_s_kernel(tc, h_attn, x, out_w_words, out_w_scales, ln_
         nc.gpsimd.memset(gamma_rows[:], 0.0)
         make_identity(nc, ident[:])
         nc.gpsimd.memset(beta_rows[:], 0.0)
-        nc.gpsimd.dma_start(out=beta_rows[0:E_CHUNKS, :], in_=ln_beta.rearrange("(c k) -> c k", k=P))
 
         def load_h(j):
             nc.sync.dma_start(out=h_sb[:, j], in_=h_attn[j].rearrange("h (p r) d -> p h (r d)", r=R))
@@ -82,6 +81,7 @@ def tile_selfattention_pa_s_kernel(tc, h_attn, x, out_w_words, out_w_scales, ln_
                 out=x_sb[:, R * j : R * (j + 1), :].rearrange("p r e -> p (r e)"),
                 in_=x[j].rearrange("(p r) e -> p (r e)", r=R),
             )
+        nc.sync.dma_start(out=beta_rows[0:E_CHUNKS, :], in_=ln_beta.rearrange("(c k) -> c k", k=P))
         gamma_sb = keep.tile([P, E], BF16)
         nc.vector.memset(one[:], 1.0)
         nc.vector.tensor_copy(out=ident_bf[:], in_=ident[:])
@@ -258,19 +258,19 @@ def tile_selfattention_pa_s_kernel(tc, h_attn, x, out_w_words, out_w_scales, ln_
         quantise(1)
         multiply(0)
         multiply(1)
-        transpose_rows(1, beta_rows)
         quantise(2)
         multiply(2)
         add_residual(0)
         quantise(3)
         multiply(3)
         nc.scalar.copy(out=gamma_sb[:], in_=gamma_all[:])
-        columns(1, beta_cols)
-        spread(beta_all, beta_cols)
+        transpose_rows(1, beta_rows)
         shift(0)
         centre(0)
         add_residual(1)
         sum_squares(0)
+        columns(1, beta_cols)
+        spread(beta_all, beta_cols)
         shift(1)
         centre(1)
         add_residual(2)

from contextlib import ExitStack

import concourse.mybir as mybir
from concourse.masks import make_identity

F32 = mybir.dt.float32
BF16 = mybir.dt.bfloat16
I32 = mybir.dt.int32
U32 = mybir.dt.uint32
U8 = mybir.dt.uint8
FP8X4 = mybir.dt.float8_e4m3fn_x4
FP4X4 = mybir.dt.float4_e2m1fn_x4
ALU = mybir.AluOpType
ACT = mybir.ActivationFunctionType

P = 128
B, H, S, D = 2, 4, 256, 128
E = H * D
R = S // P
TILES = B * R
WORDS = E // 2
E_CHUNKS = E // P
LN_EPS = 1e-6
GPSIMD_TILES = (0, 1)
SHARED_TILE = 3
SHARE = E // 2

WARM_COLS = 256
WARM_PASSES = 2

FLOPS = 2 * B * S * E * E


def tile_selfattention_pa_s_kernel(tc, h_attn, x, out_w_words, out_w_scales, ln_gamma, ln_beta, out):
    nc = tc.nc
    with ExitStack() as ctx:
        ctx.enter_context(tc.manual_schedule())
        keep = ctx.enter_context(tc.tile_pool(name="keep", bufs=1))
        work = ctx.enter_context(tc.tile_pool(name="work", bufs=TILES))
        psum = ctx.enter_context(tc.psum_pool(name="psum", bufs=TILES))
        psum_gb = ctx.enter_context(tc.psum_pool(name="psum_gb", bufs=1))

        h_sb = keep.tile([P, B, H, R * D], BF16)
        h_words = keep.tile([P, TILES, WORDS], F32)
        x_sb = keep.tile([P, TILES, E], BF16)
        w_words = keep.tile([P, 2 * E], U8, align_bytes=64)
        w_plane = keep.tile([P, E], U8, align_bytes=64)
        gamma_rows = keep.tile([P, P], BF16)
        beta_rows = keep.tile([P, P], BF16)
        ident = keep.tile([P, P], F32)
        ident_bf = keep.tile([P, P], BF16)
        one = keep.tile([P, 1], F32)
        warm = keep.tile([P, 1], F32)

        zeros = keep.tile([P, WARM_COLS], F32)
        nc.vector.memset(zeros[:], 0.0)
        scratch = psum_gb.tile([P, WARM_COLS], F32)

        def keep_clock():
            nc.tensor.matmul(out=scratch[:], lhsT=zeros[:, 0:P], rhs=zeros[:], start=True, stop=True)

        for i in range(WARM_PASSES):
            keep_clock()

        nc.vector.memset(w_plane[:].bitcast(I32), 0)
        nc.gpsimd.memset(gamma_rows[:], 0.0)
        make_identity(nc, ident[:])
        nc.gpsimd.memset(beta_rows[:], 0.0)

        def load_h(j):
            nc.sync.dma_start(out=h_sb[:, j], in_=h_attn[j].rearrange("h (p r) d -> p h (r d)", r=R))

        load_h(0)
        nc.sync.dma_start(out=gamma_rows[0:E_CHUNKS, :], in_=ln_gamma.rearrange("(c k) -> c k", k=P))
        load_h(1)
        nc.sync.dma_start(out=w_words[:].bitcast(I32), in_=out_w_words[0].bitcast(I32))
        for r in range(4):
            nc.sync.dma_start(out=w_plane[r:P:32, :].bitcast(I32), in_=out_w_scales[0, r:16:4, :].bitcast(I32))
        for j in range(B):
            nc.sync.dma_start(
                out=x_sb[:, R * j : R * (j + 1), :].rearrange("p r e -> p (r e)"),
                in_=x[j].rearrange("(p r) e -> p (r e)", r=R),
            )
        nc.sync.dma_start(out=beta_rows[0:E_CHUNKS, :], in_=ln_beta.rearrange("(c k) -> c k", k=P))
        gamma_sb = keep.tile([P, E], BF16)
        nc.vector.memset(one[:], 1.0)
        nc.vector.tensor_copy(out=ident_bf[:], in_=ident[:])
        nc.scalar.activation(out=warm[:], in_=one[:], func=ACT.Abs_reciprocal_sqrt)

        banks = []
        codes_of = []

        def gather_words(t):
            b, r = divmod(t, R)
            words = h_sb[:, b, :, r * D : (r + 1) * D].bitcast(F32)
            for u in range(2):
                nc.vector.tensor_copy(
                    out=h_words[:, t, u * P : (u + 1) * P].rearrange("p (h i) -> p h i", h=H),
                    in_=words[:, :, u : WORDS // H : 2],
                )

        def transpose_tile(t):
            bank = psum.tile([P, E], F32)
            for u in range(2):
                nc.tensor.transpose(bank[:, u * P : (u + 1) * P], h_words[:, t, u * P : (u + 1) * P], ident[:])
            banks.append(bank)

        def quantise(t):
            grouped = work.tile([P, 4 * P], BF16, align_bytes=64)
            nc.scalar.copy(
                out=grouped[:].bitcast(F32).rearrange("p (r u) -> p r u", u=2),
                in_=banks[t][:, 0 : 2 * P].rearrange("p (u r) -> p r u", u=2),
            )
            m_codes = work.tile([P, P], U32, align_bytes=64)
            m_scales = work.tile([P, P], U8, align_bytes=64)
            nc.vector.quantize_mx(out=m_codes[:].bitcast(FP8X4), scales=m_scales[:], in_=grouped[:])
            codes_of.append((m_codes, m_scales))

        def multiply(t):
            m_codes, m_scales = codes_of[t]
            nc.tensor.matmul_mx(
                out=banks[t][:],
                lhsT=m_codes[:].bitcast(FP8X4),
                lhsT_scale=m_scales[:],
                rhs=w_words[:].bitcast(FP4X4),
                rhs_scale=w_plane[:],
                start=True,
                stop=True,
            )

        rows_t = psum_gb.tile([P, 2, P], BF16)
        gamma_cols = keep.tile([P, E_CHUNKS], BF16)
        beta_cols = keep.tile([P, E_CHUNKS], BF16)
        gamma_all = psum_gb.tile([P, E], BF16)
        beta_all = psum_gb.tile([P, E], BF16)

        def transpose_rows(i, rows):
            nc.tensor.transpose(rows_t[:, i, :], rows[:], ident_bf[:])

        def columns(i, cols):
            nc.scalar.copy(out=cols[:], in_=rows_t[:, i, 0:E_CHUNKS])

        def spread(dst, cols):
            for c in range(E_CHUNKS):
                nc.tensor.transpose(dst[:, c * P : (c + 1) * P], cols[:, c : c + 1].to_broadcast([P, P]), ident_bf[:])

        y_sum = keep.tile([P, TILES], F32)
        neg_mean = keep.tile([P, TILES], F32)
        sq_sum = keep.tile([P, TILES], F32)
        rstd = keep.tile([P, TILES], F32)
        ys = []
        shifted_of = {}
        centred_of = {}

        def add_residual(t):
            y = work.tile([P, E], F32)
            nc.vector.scalar_tensor_tensor(
                out=y[:],
                in0=x_sb[:, t, :],
                scalar=-1.0 if t in GPSIMD_TILES else 1.0,
                in1=banks[t][:],
                op0=ALU.mult,
                op1=ALU.subtract if t in GPSIMD_TILES else ALU.add,
                accum_out=y_sum[:, t : t + 1],
            )
            ys.append(y)

        def shift(t):
            shifted = work.tile([P, E], F32)
            shifted_of[t] = shifted
            if t == SHARED_TILE:
                nc.scalar.activation(
                    out=shifted[:, 0:SHARE],
                    in_=ys[t][:, 0:SHARE],
                    func=ACT.Identity,
                    bias=neg_mean[:, t : t + 1],
                    scale=1.0,
                )
                return
            nc.scalar.activation(
                out=shifted[:], in_=ys[t][:], func=ACT.Identity, bias=y_sum[:, t : t + 1], scale=-1.0 * E
            )

        def sum_squares(t):
            squares = work.tile([P, E], F32)
            nc.scalar.activation(
                out=squares[:],
                in_=ys[t][:],
                func=ACT.Square,
                bias=y_sum[:, t : t + 1],
                scale=-1.0 * E,
                accum_out=sq_sum[:, t : t + 1],
            )

        def inverse_deviation(t):
            factor = E if t in GPSIMD_TILES else 1
            nc.scalar.activation(
                out=rstd[:, t : t + 1],
                in_=sq_sum[:, t : t + 1],
                func=ACT.Abs_reciprocal_sqrt,
                bias=LN_EPS * factor * factor,
                scale=float(factor * factor) / (E * E * E),
            )

        def minus_mean(t):
            nc.scalar.activation(
                out=neg_mean[:, t : t + 1], in_=y_sum[:, t : t + 1], func=ACT.Copy, scale=-1.0 / E
            )

        def centre(t):
            centred = work.tile([P, E], F32)
            centred_of[t] = centred
            own = E if t in GPSIMD_TILES else SHARE if t == SHARED_TILE else 0
            if own:
                nc.gpsimd.tensor_tensor(
                    out=centred[:, 0:own], in0=shifted_of[t][:, 0:own], in1=gamma_sb[:, 0:own], op=ALU.mult
                )
            if own < E:
                nc.vector.scalar_tensor_tensor(
                    out=centred[:, own:E],
                    in0=ys[t][:, own:E],
                    scalar=neg_mean[:, t : t + 1],
                    in1=gamma_all[:, own:E],
                    op0=ALU.add,
                    op1=ALU.mult,
                )

        def finish(t):
            b, r = divmod(t, R)
            result = work.tile([P, E], F32)
            pieces = 2 if t == TILES - 1 else 1
            width = E // pieces
            for c in range(pieces):
                cols = slice(c * width, (c + 1) * width)
                nc.vector.scalar_tensor_tensor(
                    out=result[:, cols],
                    in0=centred_of[t][:, cols],
                    scalar=rstd[:, t : t + 1],
                    in1=beta_all[:, cols],
                    op0=ALU.mult,
                    op1=ALU.add,
                )
                nc.sync.dma_start(out=out[b].rearrange("(p r) e -> p r e", r=R)[:, r, cols], in_=result[:, cols])

        gather_words(0)
        gather_words(1)
        gather_words(2)
        gather_words(3)
        transpose_tile(0)
        quantise(0)
        transpose_rows(0, gamma_rows)
        columns(0, gamma_cols)
        transpose_tile(1)
        keep_clock()
        transpose_tile(2)
        transpose_tile(3)
        spread(gamma_all, gamma_cols)
        quantise(1)
        multiply(0)
        multiply(1)
        quantise(2)
        multiply(2)
        add_residual(0)
        quantise(3)
        multiply(3)
        nc.scalar.copy(out=gamma_sb[:], in_=gamma_all[:])
        transpose_rows(1, beta_rows)
        shift(0)
        centre(0)
        add_residual(1)
        sum_squares(0)
        columns(1, beta_cols)
        spread(beta_all, beta_cols)
        shift(1)
        centre(1)
        add_residual(2)
        minus_mean(2)
        inverse_deviation(0)
        add_residual(3)
        sum_squares(2)
        minus_mean(3)
        centre(2)
        finish(0)
        inverse_deviation(2)
        sum_squares(1)
        shift(3)
        inverse_deviation(1)
        sum_squares(3)
        inverse_deviation(3)
        finish(2)
        finish(1)
        centre(3)
        finish(3)
